import numpy as np
import ml_dtypes


def mxq(x, axis, fmt="e4m3"):
    dtype, down = {"e4m3": (ml_dtypes.float8_e4m3fn, 7), "e5m2": (ml_dtypes.float8_e5m2, 14)}[fmt]
    v = np.moveaxis(np.asarray(x, np.float32).astype(ml_dtypes.bfloat16).astype(np.float64), axis, -1)
    blocks = v.reshape(v.shape[:-1] + (-1, 32))
    amax = np.abs(blocks).max(-1, keepdims=True)
    byte = np.maximum(np.where(amax > 0, np.frexp(amax)[1] - 1 + 127, 0) - down, 1)
    scale = np.exp2(byte - 127.0)
    codes = (blocks / scale).astype(np.float32).astype(dtype).astype(np.float64)
    return np.moveaxis((codes * scale).reshape(v.shape), -1, axis)


WIDE = False


def mx_kscale(k):
    if not WIDE:
        return np.ones(k)
    levels = np.array([10, -10, 5, -5, 0])
    a = np.random.permutation(np.resize(levels, k // 512 * 4)).reshape(k // 512, 4)
    idx = np.arange(k)
    return np.exp2(a[idx // 512, idx % 128 // 32])


BF16 = ml_dtypes.bfloat16


def bf(x):
    return np.asarray(x, np.float32).astype(BF16)


def f64(x):
    return np.asarray(x).astype(np.float64)


N, DIM = 2048, 128
B_COEF = 1.0
F_POW = 1
H_POW = 2


def setup_inputs():
    u = np.exp2(np.round(np.log2(mx_kscale(N)) / 2))
    r = u * np.maximum(u * u, 1.0)
    A = np.random.standard_normal((N, N)) * 1.5 / np.sqrt(N) * r[:, None] / (u * u)[None, :]
    x = (0.5 + np.random.uniform(size=(N, DIM))) * u[:, None]
    return {"A": bf(A), "x": bf(x), "t": 0}


def reference(A, x, t):
    x = f64(x)
    xh = x ** H_POW
    agg = mxq(f64(A), 1, "e4m3") @ mxq(xh, 0, "e4m3")
    return -B_COEF * x ** F_POW + agg / (xh + 1.0)

@@ -1,0 +1,181 @@
+from contextlib import ExitStack
+
+import concourse.bass as bass
+import concourse.mybir as mybir
+import concourse.tile as tile
+from concourse.masks import make_identity
+
+F32 = mybir.dt.float32
+BF16 = mybir.dt.bfloat16
+U32 = mybir.dt.uint32
+U8 = mybir.dt.uint8
+FP8X4 = mybir.dt.float8_e4m3fn_x4
+ACT = mybir.ActivationFunctionType
+ALU = mybir.AluOpType
+
+N = 2048
+DIM = 128
+P = 128
+RT = N // P
+CH = RT // 2
+PASSES = N // 512
+FLOPS = 2 * N * N * DIM
+
+V_BANKS = (3, 7, 11, 15, 19, 23)
+GROUPS = ((0, 1, 2, 3), (4, 5, 6, 7), (8, 9, 10, 11), (12, 13), (14,), (15,))
+S_EXTRA = {5: (("r", 1),), 8: (("rc", 1),), 12: (("r", 2),), 15: (("rc", 2),), 19: (("r", 3),), 22: (("rc", 3),)}
+
+
+def tile_genedynamics_kernel(tc, A, x, t, out):
+    nc = tc.nc
+    a_view = A.rearrange("(c p e) k -> p c e k", p=P, e=2)
+    x_view = x.rearrange("(c p e) d -> p c (e d)", p=P, e=2)
+    out_view = out.rearrange("(c p e) d -> p c e d", p=P, e=2)
+
+    with ExitStack() as ctx:
+        const = ctx.enter_context(tc.tile_pool(name="const", bufs=1))
+        a_pool = ctx.enter_context(tc.tile_pool(name="a", bufs=CH))
+        g_pool = ctx.enter_context(tc.tile_pool(name="grouped", bufs=4))
+        q_pool = ctx.enter_context(tc.tile_pool(name="quant", bufs=6))
+        e_pool = ctx.enter_context(tc.tile_pool(name="epi", bufs=3))
+        t_psum = ctx.enter_context(tc.psum_pool(name="tpsum", bufs=6))
+        o_psum = ctx.enter_context(tc.psum_pool(name="opsum", bufs=2))
+        ctx.enter_context(tc.manual_schedule())
+
+        ident = const.tile([P, P], F32)
+        one = const.tile([P, 1], F32)
+        warm = const.tile([P, 1], F32)
+        xs = const.tile([P, RT, DIM], BF16)
+        xh = const.tile([P, RT * DIM], F32)
+        rs = const.tile([P, RT * DIM], F32)
+        rec = const.tile([P, RT * DIM], F32)
+        xq = const.tile([P, RT * DIM], BF16, align_bytes=64)
+        x_codes = const.tile([P, PASSES * DIM], U32, align_bytes=64)
+        x_scales = const.tile([P, PASSES * DIM], U8, align_bytes=64)
+
+        xs_pairs = xs[:].rearrange("p (c e) d -> p c (e d)", e=2)
+        for h in range(2):
+            nc.sync.dma_start(out=xs_pairs[:, 4 * h : 4 * h + 4, :], in_=x_view[:, 4 * h : 4 * h + 4, :])
+        a_tiles = []
+        for c in range(CH):
+            a_sb = a_pool.tile([P, 2, N], BF16)
+            a_tiles.append(a_sb)
+            if c in (0, CH - 1):
+                for e in range(2):
+                    nc.sync.dma_start(out=a_sb[:, e, :], in_=a_view[:, c, e, :])
+            else:
+                nc.sync.dma_start(out=a_sb[:], in_=a_view[:, c, :, :])
+
+        make_identity(nc, ident[:])
+        nc.vector.memset(one[:], 1.0)
+        nc.scalar.activation(out=warm[:], in_=one[:], func=ACT.Abs_reciprocal_sqrt)
+
+        xs_flat = xs[:].rearrange("p r d -> p (r d)")
+        half = RT * DIM // 2
+        quarter = RT * DIM // 4
+        for h in range(2):
+            cols = slice(h * half, (h + 1) * half)
+            nc.scalar.activation(out=xh[:, cols], in_=xs_flat[:, cols], func=ACT.Square)
+            src = xs[:, 8 * h : 8 * h + 8, :].rearrange("p (g t) d -> p g d t", t=4)
+            nc.vector.tensor_tensor(
+                out=xq[:, cols].rearrange("p (g d t) -> p g d t", g=2, t=4), in0=src, in1=src, op=ALU.mult
+            )
+        nc.vector.quantize_mx(out=x_codes[:].bitcast(FP8X4), scales=x_scales[:], in_=xq[:])
+
+        def recip_step(kind, q):
+            cols = slice(q * quarter, (q + 1) * quarter)
+            if kind == "r":
+                nc.scalar.activation(out=rs[:, cols], in_=xh[:, cols], func=ACT.Abs_reciprocal_sqrt, bias=1.0, scale=1.0)
+            else:
+                nc.scalar.activation(out=rec[:, cols], in_=rs[:, cols], func=ACT.Square)
+
+        recip_step("r", 0)
+        recip_step("rc", 0)
+
+        grouped = {}
+        codes = {}
+        scales = {}
+        acc = {}
+        group_of = {}
+        for b, rows in enumerate(GROUPS):
+            for n in rows:
+                group_of[n] = b
+
+        def transposes_and_copies(n):
+            a32 = a_tiles[n // 2][:, n % 2, :].bitcast(F32)
+            grp = g_pool.tile([P, N], BF16, align_bytes=64)
+            grouped[n] = grp
+            for h in range(2):
+                tp = t_psum.tile([P, 512], F32)
+                for j in range(4):
+                    w = 4 * h + j
+                    nc.tensor.transpose(tp[:, j * P : (j + 1) * P], a32[:, w * P : (w + 1) * P], ident[:])
+                dst = grp[:, h * 1024 : (h + 1) * 1024].bitcast(F32).rearrange("p (g i u) -> p g i u", g=2, u=2)
+                src = tp[:].rearrange("p (g u i) -> p g i u", g=2, u=2)
+                bank = 2 * n + h
+                if bank in V_BANKS:
+                    nc.vector.tensor_copy(out=dst, in_=src)
+                else:
+                    nc.scalar.copy(out=dst, in_=src)
+                for kind, q in S_EXTRA.get(bank, ()):
+                    recip_step(kind, q)
+
+        def quantise(n):
+            cd = q_pool.tile([P, 512], U32, align_bytes=64)
+            sc = q_pool.tile([P, 512], U8, align_bytes=64)
+            codes[n] = cd
+            scales[n] = sc
+            nc.vector.quantize_mx(out=cd[:].bitcast(FP8X4), scales=sc[:], in_=grouped[n][:])
+
+        def mx_passes(n):
+            b = group_of[n]
+            rows = GROUPS[b]
+            if n == rows[0]:
+                ps = o_psum.tile([P, 512], F32)
+                acc[b] = ps
+            o = (n - rows[0]) * DIM
+            for g in range(PASSES):
+                cols = slice(g * P, (g + 1) * P)
+                nc.tensor.matmul_mx(
+                    out=acc[b][:, o : o + DIM],
+                    lhsT=codes[n][:, cols].bitcast(FP8X4),
+                    lhsT_scale=scales[n][:, cols],
+                    rhs=x_codes[:, cols].bitcast(FP8X4),
+                    rhs_scale=x_scales[:, cols],
+                    start=(g == 0),
+                    stop=(g == PASSES - 1),
+                )
+
+        def epilogue(b):
+            rows = GROUPS[b]
+            width = len(rows) * DIM
+            cols = slice(rows[0] * DIM, rows[0] * DIM + width)
+            prod = e_pool.tile([P, 512], F32)
+            res = e_pool.tile([P, 512], F32)
+            nc.vector.tensor_tensor(out=prod[:, :width], in0=acc[b][:, :width], in1=rec[:, cols], op=ALU.mult)
+            nc.vector.tensor_tensor(out=res[:, :width], in0=prod[:, :width], in1=xs_flat[:, cols], op=ALU.subtract)
+            if len(rows) == 1:
+                n = rows[0]
+                nc.sync.dma_start(out=out_view[:, n // 2, n % 2, :], in_=res[:, :width])
+            else:
+                c0 = rows[0] // 2
+                nc.sync.dma_start(
+                    out=out_view[:, c0 : c0 + len(rows) // 2, :, :].rearrange("p c e d -> p c (e d)"),
+                    in_=res[:, :width].rearrange("p (c f) -> p c f", f=2 * DIM),
+                )
+
+        for c in range(CH):
+            transposes_and_copies(2 * c)
+            transposes_and_copies(2 * c + 1)
+            if c >= 1:
+                mx_passes(2 * c - 2)
+                mx_passes(2 * c - 1)
+            quantise(2 * c)
+            quantise(2 * c + 1)
+            if c >= 2 and c % 2 == 0:
+                epilogue(c // 2 - 1)
+        mx_passes(14)
+        epilogue(3)
+        mx_passes(15)
+        epilogue(4)
+        epilogue(5)

@@ -23,6 +23,7 @@ FLOPS = 2 * N * N * DIM
 
 V_BANKS = (3, 7, 11, 15, 19, 23)
 GROUPS = ((0, 1, 2, 3), (4, 5, 6, 7), (8, 9, 10, 11), (12, 13), (14,), (15,))
+WARM = (3, 1, 4)
 S_EXTRA = {5: (("r", 1),), 8: (("rc", 1),), 12: (("r", 2),), 15: (("rc", 2),), 19: (("r", 3),), 22: (("rc", 3),)}
 
 
@@ -91,6 +92,15 @@ def tile_genedynamics_kernel(tc, A, x, t, out):
 
         recip_step("r", 0)
         recip_step("rc", 0)
+
+        warm_ps = t_psum.tile([P, 512], F32, tag="tp")
+        xs_words = xs_flat.bitcast(F32)
+
+        def keep_clock(count):
+            for i in range(count):
+                nc.tensor.matmul(warm_ps[:, 0:P], lhsT=ident[:], rhs=xs_words[:, 0:P], start=True, stop=True)
+
+        keep_clock(WARM[0])
 
         grouped = {}
         codes = {}
@@ -166,7 +176,11 @@ def tile_genedynamics_kernel(tc, A, x, t, out):
 
         for c in range(CH):
             transposes_and_copies(2 * c)
+            if c == 0:
+                keep_clock(WARM[1])
             transposes_and_copies(2 * c + 1)
+            if c == 0:
+                keep_clock(WARM[2])
             if c >= 1:
                 mx_passes(2 * c - 2)
                 mx_passes(2 * c - 1)

@@ -1,8 +1,6 @@
 from contextlib import ExitStack
 
-import concourse.bass as bass
 import concourse.mybir as mybir
-import concourse.tile as tile
 from concourse.masks import make_identity
 
 F32 = mybir.dt.float32
@@ -21,24 +19,24 @@ CH = RT // 2
 PASSES = N // 512
 FLOPS = 2 * N * N * DIM
 
-V_BANKS = (3, 7, 11, 15, 19, 23)
-GROUPS = ((0, 1, 2, 3), (4, 5, 6, 7), (8, 9, 10, 11), (12, 13), (14,), (15,))
-WARM = (3, 1, 4)
-S_EXTRA = {5: (("r", 1),), 8: (("rc", 1),), 12: (("r", 2),), 15: (("rc", 2),), 19: (("r", 3),), 22: (("rc", 3),)}
+V_BANKS = (0, 1, 3, 4, 6, 10, 14, 17, 25)
+S_EXTRA = {2: ("r", 2), 5: ("r", 3), 7: ("rc", 2), 9: ("rc", 3)}
+LAST_WOVEN = 5
 
 
 def tile_genedynamics_kernel(tc, A, x, t, out):
     nc = tc.nc
     a_view = A.rearrange("(c p e) k -> p c e k", p=P, e=2)
     x_view = x.rearrange("(c p e) d -> p c (e d)", p=P, e=2)
-    out_view = out.rearrange("(c p e) d -> p c e d", p=P, e=2)
+    out_view = out.rearrange("(c p e) d -> p c (e d)", p=P, e=2)
 
     with ExitStack() as ctx:
         const = ctx.enter_context(tc.tile_pool(name="const", bufs=1))
         a_pool = ctx.enter_context(tc.tile_pool(name="a", bufs=CH))
-        g_pool = ctx.enter_context(tc.tile_pool(name="grouped", bufs=4))
-        q_pool = ctx.enter_context(tc.tile_pool(name="quant", bufs=6))
-        e_pool = ctx.enter_context(tc.tile_pool(name="epi", bufs=3))
+        g_pool = ctx.enter_context(tc.tile_pool(name="grouped", bufs=6))
+        q_pool = ctx.enter_context(tc.tile_pool(name="quant", bufs=8))
+        p_pool = ctx.enter_context(tc.tile_pool(name="prod", bufs=4))
+        r_pool = ctx.enter_context(tc.tile_pool(name="res", bufs=CH))
         t_psum = ctx.enter_context(tc.psum_pool(name="tpsum", bufs=6))
         o_psum = ctx.enter_context(tc.psum_pool(name="opsum", bufs=2))
         ctx.enter_context(tc.manual_schedule())
@@ -81,7 +79,6 @@ def tile_genedynamics_kernel(tc, A, x, t, out):
             nc.vector.tensor_tensor(
                 out=xq[:, cols].rearrange("p (g d t) -> p g d t", g=2, t=4), in0=src, in1=src, op=ALU.mult
             )
-        nc.vector.quantize_mx(out=x_codes[:].bitcast(FP8X4), scales=x_scales[:], in_=xq[:])
 
         def recip_step(kind, q):
             cols = slice(q * quarter, (q + 1) * quarter)
@@ -91,25 +88,15 @@ def tile_genedynamics_kernel(tc, A, x, t, out):
                 nc.scalar.activation(out=rec[:, cols], in_=rs[:, cols], func=ACT.Square)
 
         recip_step("r", 0)
+        recip_step("r", 1)
         recip_step("rc", 0)
-
-        warm_ps = t_psum.tile([P, 512], F32, tag="tp")
-        xs_words = xs_flat.bitcast(F32)
-
-        def keep_clock(count):
-            for i in range(count):
-                nc.tensor.matmul(warm_ps[:, 0:P], lhsT=ident[:], rhs=xs_words[:, 0:P], start=True, stop=True)
-
-        keep_clock(WARM[0])
+        recip_step("rc", 1)
 
         grouped = {}
         codes = {}
         scales = {}
         acc = {}
-        group_of = {}
-        for b, rows in enumerate(GROUPS):
-            for n in rows:
-                group_of[n] = b
+        prods = {}
 
         def transposes_and_copies(n):
             a32 = a_tiles[n // 2][:, n % 2, :].bitcast(F32)
@@ -127,69 +114,76 @@ def tile_genedynamics_kernel(tc, A, x, t, out):
                     nc.vector.tensor_copy(out=dst, in_=src)
                 else:
                     nc.scalar.copy(out=dst, in_=src)
-                for kind, q in S_EXTRA.get(bank, ()):
-                    recip_step(kind, q)
+                if bank in S_EXTRA:
+                    recip_step(S_EXTRA[bank][0], S_EXTRA[bank][1])
 
-        def quantise(n):
+        def quantise(n, pieces):
             cd = q_pool.tile([P, 512], U32, align_bytes=64)
             sc = q_pool.tile([P, 512], U8, align_bytes=64)
             codes[n] = cd
             scales[n] = sc
-            nc.vector.quantize_mx(out=cd[:].bitcast(FP8X4), scales=sc[:], in_=grouped[n][:])
-
-        def mx_passes(n):
-            b = group_of[n]
-            rows = GROUPS[b]
-            if n == rows[0]:
-                ps = o_psum.tile([P, 512], F32)
-                acc[b] = ps
-            o = (n - rows[0]) * DIM
-            for g in range(PASSES):
-                cols = slice(g * P, (g + 1) * P)
-                nc.tensor.matmul_mx(
-                    out=acc[b][:, o : o + DIM],
-                    lhsT=codes[n][:, cols].bitcast(FP8X4),
-                    lhsT_scale=scales[n][:, cols],
-                    rhs=x_codes[:, cols].bitcast(FP8X4),
-                    rhs_scale=x_scales[:, cols],
-                    start=(g == 0),
-                    stop=(g == PASSES - 1),
+            width = 512 // pieces
+            for i in range(pieces):
+                cols = slice(i * width, (i + 1) * width)
+                nc.vector.quantize_mx(
+                    out=cd[:, cols].bitcast(FP8X4),
+                    scales=sc[:, cols],
+                    in_=grouped[n][:, 4 * i * width : 4 * (i + 1) * width],
                 )
 
-        def epilogue(b):
-            rows = GROUPS[b]
-            width = len(rows) * DIM
-            cols = slice(rows[0] * DIM, rows[0] * DIM + width)
-            prod = e_pool.tile([P, 512], F32)
-            res = e_pool.tile([P, 512], F32)
-            nc.vector.tensor_tensor(out=prod[:, :width], in0=acc[b][:, :width], in1=rec[:, cols], op=ALU.mult)
-            nc.vector.tensor_tensor(out=res[:, :width], in0=prod[:, :width], in1=xs_flat[:, cols], op=ALU.subtract)
-            if len(rows) == 1:
-                n = rows[0]
-                nc.sync.dma_start(out=out_view[:, n // 2, n % 2, :], in_=res[:, :width])
-            else:
-                c0 = rows[0] // 2
-                nc.sync.dma_start(
-                    out=out_view[:, c0 : c0 + len(rows) // 2, :, :].rearrange("p c e d -> p c (e d)"),
-                    in_=res[:, :width].rearrange("p (c f) -> p c f", f=2 * DIM),
-                )
+        def products(c):
+            ps = o_psum.tile([P, 2 * DIM], F32)
+            acc[c] = ps
+            for e in range(2):
+                n = 2 * c + e
+                for g in range(PASSES):
+                    cols = slice(g * P, (g + 1) * P)
+                    nc.tensor.matmul_mx(
+                        out=ps[:, e * DIM : (e + 1) * DIM],
+                        lhsT=codes[n][:, cols].bitcast(FP8X4),
+                        lhsT_scale=scales[n][:, cols],
+                        rhs=x_codes[:, cols].bitcast(FP8X4),
+                        rhs_scale=x_scales[:, cols],
+                        start=(g == 0),
+                        stop=(g == PASSES - 1),
+                    )
+
+        def divide(c):
+            cols = slice(2 * c * DIM, 2 * (c + 1) * DIM)
+            prod = p_pool.tile([P, 2 * DIM], F32)
+            prods[c] = prod
+            nc.vector.tensor_tensor(out=prod[:], in0=acc[c][:], in1=rec[:, cols], op=ALU.mult)
+
+        def subtract_and_store(c):
+            cols = slice(2 * c * DIM, 2 * (c + 1) * DIM)
+            res = r_pool.tile([P, 2 * DIM], F32)
+            nc.vector.tensor_tensor(out=res[:], in0=prods[c][:], in1=xs_flat[:, cols], op=ALU.subtract)
+            nc.sync.dma_start(out=out_view[:, c, :], in_=res[:])
 
         for c in range(CH):
             transposes_and_copies(2 * c)
             if c == 0:
-                keep_clock(WARM[1])
+                nc.vector.quantize_mx(out=x_codes[:].bitcast(FP8X4), scales=x_scales[:], in_=xq[:])
             transposes_and_copies(2 * c + 1)
-            if c == 0:
-                keep_clock(WARM[2])
-            if c >= 1:
-                mx_passes(2 * c - 2)
-                mx_passes(2 * c - 1)
-            quantise(2 * c)
-            quantise(2 * c + 1)
-            if c >= 2 and c % 2 == 0:
-                epilogue(c // 2 - 1)
-        mx_passes(14)
-        epilogue(3)
-        mx_passes(15)
-        epilogue(4)
-        epilogue(5)
+            if 1 <= c <= LAST_WOVEN:
+                products(c - 1)
+            if c == CH - 1:
+                products(c - 2)
+                quantise(2 * c, 1)
+                divide(c - 2)
+                quantise(2 * c + 1, 2)
+            else:
+                if c >= 2:
+                    divide(c - 2)
+                quantise(2 * c, 1)
+                if 2 <= c <= LAST_WOVEN:
+                    subtract_and_store(c - 2)
+                quantise(2 * c + 1, 1)
+        products(CH - 2)
+        products(CH - 1)
+        subtract_and_store(CH - 4)
+        divide(CH - 2)
+        subtract_and_store(CH - 3)
+        divide(CH - 1)
+        subtract_and_store(CH - 2)
+        subtract_and_store(CH - 1)

@@ -22,13 +22,14 @@ FLOPS = 2 * N * N * DIM
 V_BANKS = (0, 1, 3, 4, 6, 10, 14, 17, 25)
 S_EXTRA = {2: ("r", 2), 5: ("r", 3), 7: ("rc", 2), 9: ("rc", 3)}
 LAST_WOVEN = 5
+GROUPS = ((0, 1), (2, 3), (4, 5), (6, 7), (8, 9), (10, 11), (12, 13), (14,), (15,))
 
 
 def tile_genedynamics_kernel(tc, A, x, t, out):
     nc = tc.nc
     a_view = A.rearrange("(c p e) k -> p c e k", p=P, e=2)
     x_view = x.rearrange("(c p e) d -> p c (e d)", p=P, e=2)
-    out_view = out.rearrange("(c p e) d -> p c (e d)", p=P, e=2)
+    out_view = out.rearrange("(c p e) d -> p c e d", p=P, e=2)
 
     with ExitStack() as ctx:
         const = ctx.enter_context(tc.tile_pool(name="const", bufs=1))
@@ -36,7 +37,7 @@ def tile_genedynamics_kernel(tc, A, x, t, out):
         g_pool = ctx.enter_context(tc.tile_pool(name="grouped", bufs=6))
         q_pool = ctx.enter_context(tc.tile_pool(name="quant", bufs=8))
         p_pool = ctx.enter_context(tc.tile_pool(name="prod", bufs=4))
-        r_pool = ctx.enter_context(tc.tile_pool(name="res", bufs=CH))
+        r_pool = ctx.enter_context(tc.tile_pool(name="res", bufs=len(GROUPS)))
         t_psum = ctx.enter_context(tc.psum_pool(name="tpsum", bufs=6))
         o_psum = ctx.enter_context(tc.psum_pool(name="opsum", bufs=2))
         ctx.enter_context(tc.manual_schedule())
@@ -131,11 +132,14 @@ def tile_genedynamics_kernel(tc, A, x, t, out):
                     in_=grouped[n][:, 4 * i * width : 4 * (i + 1) * width],
                 )
 
-        def products(c):
-            ps = o_psum.tile([P, 2 * DIM], F32)
-            acc[c] = ps
-            for e in range(2):
-                n = 2 * c + e
+        def products(b):
+            rows = GROUPS[b]
+            if b == len(GROUPS) - 1:
+                ps = t_psum.tile([P, 512], F32, tag="tp")
+            else:
+                ps = o_psum.tile([P, 2 * DIM], F32)
+            acc[b] = ps
+            for e, n in enumerate(rows):
                 for g in range(PASSES):
                     cols = slice(g * P, (g + 1) * P)
                     nc.tensor.matmul_mx(
@@ -148,17 +152,26 @@ def tile_genedynamics_kernel(tc, A, x, t, out):
                         stop=(g == PASSES - 1),
                     )
 
-        def divide(c):
-            cols = slice(2 * c * DIM, 2 * (c + 1) * DIM)
+        def divide(b):
+            rows = GROUPS[b]
+            width = len(rows) * DIM
+            cols = slice(rows[0] * DIM, rows[0] * DIM + width)
             prod = p_pool.tile([P, 2 * DIM], F32)
-            prods[c] = prod
-            nc.vector.tensor_tensor(out=prod[:], in0=acc[c][:], in1=rec[:, cols], op=ALU.mult)
+            prods[b] = prod
+            nc.vector.tensor_tensor(out=prod[:, :width], in0=acc[b][:, :width], in1=rec[:, cols], op=ALU.mult)
 
-        def subtract_and_store(c):
-            cols = slice(2 * c * DIM, 2 * (c + 1) * DIM)
+        def subtract_and_store(b):
+            rows = GROUPS[b]
+            width = len(rows) * DIM
+            cols = slice(rows[0] * DIM, rows[0] * DIM + width)
             res = r_pool.tile([P, 2 * DIM], F32)
-            nc.vector.tensor_tensor(out=res[:], in0=prods[c][:], in1=xs_flat[:, cols], op=ALU.subtract)
-            nc.sync.dma_start(out=out_view[:, c, :], in_=res[:])
+            nc.vector.tensor_tensor(out=res[:, :width], in0=prods[b][:, :width], in1=xs_flat[:, cols], op=ALU.subtract)
+            if len(rows) == 2:
+                nc.sync.dma_start(
+                    out=out_view[:, rows[0] // 2, :, :], in_=res[:].rearrange("p (e d) -> p e d", d=DIM)
+                )
+            else:
+                nc.sync.dma_start(out=out_view[:, rows[0] // 2, rows[0] % 2, :], in_=res[:, :DIM])
 
         for c in range(CH):
             transposes_and_copies(2 * c)
@@ -179,11 +192,15 @@ def tile_genedynamics_kernel(tc, A, x, t, out):
                 if 2 <= c <= LAST_WOVEN:
                     subtract_and_store(c - 2)
                 quantise(2 * c + 1, 1)
-        products(CH - 2)
-        products(CH - 1)
-        subtract_and_store(CH - 4)
-        divide(CH - 2)
-        subtract_and_store(CH - 3)
-        divide(CH - 1)
-        subtract_and_store(CH - 2)
-        subtract_and_store(CH - 1)
+                if c == CH - 2:
+                    subtract_and_store(c - 2)
+        products(6)
+        products(7)
+        products(8)
+        divide(6)
+        subtract_and_store(5)
+        divide(7)
+        subtract_and_store(6)
+        divide(8)
+        subtract_and_store(7)
+        subtract_and_store(8)

@@ -14,30 +14,32 @@ ALU = mybir.AluOpType
 N = 2048
 DIM = 128
 P = 128
-RT = N // P
-CH = RT // 2
-PASSES = N // 512
+ROW_TILES = N // P
+CHUNKS = ROW_TILES // 2
+K_PASS = 4 * P
+PASSES = N // K_PASS
+BANK = 512
+X_COLS = ROW_TILES * DIM
 FLOPS = 2 * N * N * DIM
 
-V_BANKS = (0, 1, 3, 4, 6, 10, 14, 17, 25)
-S_EXTRA = {2: ("r", 2), 5: ("r", 3), 7: ("rc", 2), 9: ("rc", 3)}
+VECTOR_BANKS = (0, 1, 3, 4, 6, 10, 25)
+RECIPROCAL_AFTER_BANK = {2: ("rsqrt", 2), 5: ("rsqrt", 3), 7: ("square", 2), 9: ("square", 3)}
 LAST_WOVEN = 5
-GROUPS = ((0, 1), (2, 3), (4, 5), (6, 7), (8, 9), (10, 11), (12, 13), (14,), (15,))
 
 
 def tile_genedynamics_kernel(tc, A, x, t, out):
     nc = tc.nc
     a_view = A.rearrange("(c p e) k -> p c e k", p=P, e=2)
     x_view = x.rearrange("(c p e) d -> p c (e d)", p=P, e=2)
-    out_view = out.rearrange("(c p e) d -> p c e d", p=P, e=2)
+    out_view = out.rearrange("(c p e) d -> p c (e d)", p=P, e=2)
 
     with ExitStack() as ctx:
         const = ctx.enter_context(tc.tile_pool(name="const", bufs=1))
-        a_pool = ctx.enter_context(tc.tile_pool(name="a", bufs=CH))
+        a_pool = ctx.enter_context(tc.tile_pool(name="a", bufs=CHUNKS))
         g_pool = ctx.enter_context(tc.tile_pool(name="grouped", bufs=6))
         q_pool = ctx.enter_context(tc.tile_pool(name="quant", bufs=8))
         p_pool = ctx.enter_context(tc.tile_pool(name="prod", bufs=4))
-        r_pool = ctx.enter_context(tc.tile_pool(name="res", bufs=len(GROUPS)))
+        r_pool = ctx.enter_context(tc.tile_pool(name="res", bufs=CHUNKS))
         t_psum = ctx.enter_context(tc.psum_pool(name="tpsum", bufs=6))
         o_psum = ctx.enter_context(tc.psum_pool(name="opsum", bufs=2))
         ctx.enter_context(tc.manual_schedule())
@@ -45,22 +47,23 @@ def tile_genedynamics_kernel(tc, A, x, t, out):
         ident = const.tile([P, P], F32)
         one = const.tile([P, 1], F32)
         warm = const.tile([P, 1], F32)
-        xs = const.tile([P, RT, DIM], BF16)
-        xh = const.tile([P, RT * DIM], F32)
-        rs = const.tile([P, RT * DIM], F32)
-        rec = const.tile([P, RT * DIM], F32)
-        xq = const.tile([P, RT * DIM], BF16, align_bytes=64)
+        xs = const.tile([P, ROW_TILES, DIM], BF16)
+        xh = const.tile([P, X_COLS], F32)
+        rs = const.tile([P, X_COLS], F32)
+        rec = const.tile([P, X_COLS], F32)
+        xq = const.tile([P, X_COLS], BF16, align_bytes=64)
         x_codes = const.tile([P, PASSES * DIM], U32, align_bytes=64)
         x_scales = const.tile([P, PASSES * DIM], U8, align_bytes=64)
 
         xs_pairs = xs[:].rearrange("p (c e) d -> p c (e d)", e=2)
-        for h in range(2):
-            nc.sync.dma_start(out=xs_pairs[:, 4 * h : 4 * h + 4, :], in_=x_view[:, 4 * h : 4 * h + 4, :])
+        for part in range(2):
+            chunks = slice(part * CHUNKS // 2, (part + 1) * CHUNKS // 2)
+            nc.sync.dma_start(out=xs_pairs[:, chunks, :], in_=x_view[:, chunks, :])
         a_tiles = []
-        for c in range(CH):
+        for c in range(CHUNKS):
             a_sb = a_pool.tile([P, 2, N], BF16)
             a_tiles.append(a_sb)
-            if c in (0, CH - 1):
+            if c in (0, CHUNKS - 1):
                 for e in range(2):
                     nc.sync.dma_start(out=a_sb[:, e, :], in_=a_view[:, c, e, :])
             else:
@@ -70,28 +73,34 @@ def tile_genedynamics_kernel(tc, A, x, t, out):
         nc.vector.memset(one[:], 1.0)
         nc.scalar.activation(out=warm[:], in_=one[:], func=ACT.Abs_reciprocal_sqrt)
 
-        xs_flat = xs[:].rearrange("p r d -> p (r d)")
-        half = RT * DIM // 2
-        quarter = RT * DIM // 4
-        for h in range(2):
-            cols = slice(h * half, (h + 1) * half)
+        xs_flat = xs[:].rearrange("p n d -> p (n d)")
+        half = X_COLS // 2
+        quarter = X_COLS // 4
+        for part in range(2):
+            cols = slice(part * half, (part + 1) * half)
             nc.scalar.activation(out=xh[:, cols], in_=xs_flat[:, cols], func=ACT.Square)
-            src = xs[:, 8 * h : 8 * h + 8, :].rearrange("p (g t) d -> p g d t", t=4)
+            tiles = slice(part * ROW_TILES // 2, (part + 1) * ROW_TILES // 2)
+            x_rows = xs[:, tiles, :].rearrange("p (g slot) d -> p g d slot", slot=4)
             nc.vector.tensor_tensor(
-                out=xq[:, cols].rearrange("p (g d t) -> p g d t", g=2, t=4), in0=src, in1=src, op=ALU.mult
+                out=xq[:, cols].rearrange("p (g d slot) -> p g d slot", g=PASSES // 2, slot=4),
+                in0=x_rows,
+                in1=x_rows,
+                op=ALU.mult,
             )
 
-        def recip_step(kind, q):
+        def reciprocal_step(step, q):
             cols = slice(q * quarter, (q + 1) * quarter)
-            if kind == "r":
-                nc.scalar.activation(out=rs[:, cols], in_=xh[:, cols], func=ACT.Abs_reciprocal_sqrt, bias=1.0, scale=1.0)
+            if step == "rsqrt":
+                nc.scalar.activation(
+                    out=rs[:, cols], in_=xh[:, cols], func=ACT.Abs_reciprocal_sqrt, bias=1.0, scale=1.0
+                )
             else:
                 nc.scalar.activation(out=rec[:, cols], in_=rs[:, cols], func=ACT.Square)
 
-        recip_step("r", 0)
-        recip_step("r", 1)
-        recip_step("rc", 0)
-        recip_step("rc", 1)
+        reciprocal_step("rsqrt", 0)
+        reciprocal_step("rsqrt", 1)
+        reciprocal_step("square", 0)
+        reciprocal_step("square", 1)
 
         grouped = {}
         codes = {}
@@ -104,42 +113,39 @@ def tile_genedynamics_kernel(tc, A, x, t, out):
             grp = g_pool.tile([P, N], BF16, align_bytes=64)
             grouped[n] = grp
             for h in range(2):
-                tp = t_psum.tile([P, 512], F32)
+                tp = t_psum.tile([P, BANK], F32)
                 for j in range(4):
                     w = 4 * h + j
                     nc.tensor.transpose(tp[:, j * P : (j + 1) * P], a32[:, w * P : (w + 1) * P], ident[:])
-                dst = grp[:, h * 1024 : (h + 1) * 1024].bitcast(F32).rearrange("p (g i u) -> p g i u", g=2, u=2)
+                dst = grp[:, 2 * h * BANK : 2 * (h + 1) * BANK].bitcast(F32).rearrange("p (g i u) -> p g i u", g=2, u=2)
                 src = tp[:].rearrange("p (g u i) -> p g i u", g=2, u=2)
                 bank = 2 * n + h
-                if bank in V_BANKS:
+                if bank in VECTOR_BANKS:
                     nc.vector.tensor_copy(out=dst, in_=src)
                 else:
                     nc.scalar.copy(out=dst, in_=src)
-                if bank in S_EXTRA:
-                    recip_step(S_EXTRA[bank][0], S_EXTRA[bank][1])
+                if bank in RECIPROCAL_AFTER_BANK:
+                    reciprocal_step(RECIPROCAL_AFTER_BANK[bank][0], RECIPROCAL_AFTER_BANK[bank][1])
 
         def quantise(n, pieces):
-            cd = q_pool.tile([P, 512], U32, align_bytes=64)
-            sc = q_pool.tile([P, 512], U8, align_bytes=64)
+            cd = q_pool.tile([P, PASSES * P], U32, align_bytes=64)
+            sc = q_pool.tile([P, PASSES * P], U8, align_bytes=64)
             codes[n] = cd
             scales[n] = sc
-            width = 512 // pieces
-            for i in range(pieces):
-                cols = slice(i * width, (i + 1) * width)
+            width = PASSES * P // pieces
+            for piece in range(pieces):
+                cols = slice(piece * width, (piece + 1) * width)
                 nc.vector.quantize_mx(
                     out=cd[:, cols].bitcast(FP8X4),
                     scales=sc[:, cols],
-                    in_=grouped[n][:, 4 * i * width : 4 * (i + 1) * width],
+                    in_=grouped[n][:, 4 * piece * width : 4 * (piece + 1) * width],
                 )
 
-        def products(b):
-            rows = GROUPS[b]
-            if b == len(GROUPS) - 1:
-                ps = t_psum.tile([P, 512], F32, tag="tp")
-            else:
-                ps = o_psum.tile([P, 2 * DIM], F32)
-            acc[b] = ps
-            for e, n in enumerate(rows):
+        def products(c):
+            ps = o_psum.tile([P, 2 * DIM], F32)
+            acc[c] = ps
+            for e in range(2):
+                n = 2 * c + e
                 for g in range(PASSES):
                     cols = slice(g * P, (g + 1) * P)
                     nc.tensor.matmul_mx(
@@ -152,35 +158,26 @@ def tile_genedynamics_kernel(tc, A, x, t, out):
                         stop=(g == PASSES - 1),
                     )
 
-        def divide(b):
-            rows = GROUPS[b]
-            width = len(rows) * DIM
-            cols = slice(rows[0] * DIM, rows[0] * DIM + width)
+        def divide(c):
+            cols = slice(2 * c * DIM, 2 * (c + 1) * DIM)
             prod = p_pool.tile([P, 2 * DIM], F32)
-            prods[b] = prod
-            nc.vector.tensor_tensor(out=prod[:, :width], in0=acc[b][:, :width], in1=rec[:, cols], op=ALU.mult)
+            prods[c] = prod
+            nc.vector.tensor_tensor(out=prod[:], in0=acc[c][:], in1=rec[:, cols], op=ALU.mult)
 
-        def subtract_and_store(b):
-            rows = GROUPS[b]
-            width = len(rows) * DIM
-            cols = slice(rows[0] * DIM, rows[0] * DIM + width)
+        def subtract_and_store(c):
+            cols = slice(2 * c * DIM, 2 * (c + 1) * DIM)
             res = r_pool.tile([P, 2 * DIM], F32)
-            nc.vector.tensor_tensor(out=res[:, :width], in0=prods[b][:, :width], in1=xs_flat[:, cols], op=ALU.subtract)
-            if len(rows) == 2:
-                nc.sync.dma_start(
-                    out=out_view[:, rows[0] // 2, :, :], in_=res[:].rearrange("p (e d) -> p e d", d=DIM)
-                )
-            else:
-                nc.sync.dma_start(out=out_view[:, rows[0] // 2, rows[0] % 2, :], in_=res[:, :DIM])
+            nc.vector.tensor_tensor(out=res[:], in0=prods[c][:], in1=xs_flat[:, cols], op=ALU.subtract)
+            nc.sync.dma_start(out=out_view[:, c, :], in_=res[:])
 
-        for c in range(CH):
+        for c in range(CHUNKS):
             transposes_and_copies(2 * c)
             if c == 0:
                 nc.vector.quantize_mx(out=x_codes[:].bitcast(FP8X4), scales=x_scales[:], in_=xq[:])
             transposes_and_copies(2 * c + 1)
             if 1 <= c <= LAST_WOVEN:
                 products(c - 1)
-            if c == CH - 1:
+            if c == CHUNKS - 1:
                 products(c - 2)
                 quantise(2 * c, 1)
                 divide(c - 2)
@@ -192,15 +189,11 @@ def tile_genedynamics_kernel(tc, A, x, t, out):
                 if 2 <= c <= LAST_WOVEN:
                     subtract_and_store(c - 2)
                 quantise(2 * c + 1, 1)
-                if c == CH - 2:
-                    subtract_and_store(c - 2)
-        products(6)
-        products(7)
-        products(8)
-        divide(6)
-        subtract_and_store(5)
-        divide(7)
-        subtract_and_store(6)
-        divide(8)
-        subtract_and_store(7)
-        subtract_and_store(8)
+        products(CHUNKS - 2)
+        products(CHUNKS - 1)
+        subtract_and_store(CHUNKS - 4)
+        divide(CHUNKS - 2)
+        subtract_and_store(CHUNKS - 3)
+        divide(CHUNKS - 1)
+        subtract_and_store(CHUNKS - 2)
+        subtract_and_store(CHUNKS - 1)

from contextlib import ExitStack

import concourse.mybir as mybir
from concourse.masks import make_identity

F32 = mybir.dt.float32
BF16 = mybir.dt.bfloat16
U32 = mybir.dt.uint32
U8 = mybir.dt.uint8
FP8X4 = mybir.dt.float8_e4m3fn_x4
ACT = mybir.ActivationFunctionType
ALU = mybir.AluOpType

N = 2048
DIM = 128
P = 128
ROW_TILES = N // P
CHUNKS = ROW_TILES // 2
K_PASS = 4 * P
PASSES = N // K_PASS
BANK = 512
X_COLS = ROW_TILES * DIM
FLOPS = 2 * N * N * DIM

VECTOR_BANKS = (0, 1, 3, 4, 6, 10, 25)
RECIPROCAL_AFTER_BANK = {2: ("rsqrt", 2), 5: ("rsqrt", 3), 7: ("square", 2), 9: ("square", 3)}
LAST_WOVEN = 5


def tile_genedynamics_kernel(tc, A, x, t, out):
    nc = tc.nc
    a_view = A.rearrange("(c p e) k -> p c e k", p=P, e=2)
    x_view = x.rearrange("(c p e) d -> p c (e d)", p=P, e=2)
    out_view = out.rearrange("(c p e) d -> p c (e d)", p=P, e=2)

    with ExitStack() as ctx:
        const = ctx.enter_context(tc.tile_pool(name="const", bufs=1))
        a_pool = ctx.enter_context(tc.tile_pool(name="a", bufs=CHUNKS))
        g_pool = ctx.enter_context(tc.tile_pool(name="grouped", bufs=6))
        q_pool = ctx.enter_context(tc.tile_pool(name="quant", bufs=8))
        p_pool = ctx.enter_context(tc.tile_pool(name="prod", bufs=4))
        r_pool = ctx.enter_context(tc.tile_pool(name="res", bufs=CHUNKS))
        t_psum = ctx.enter_context(tc.psum_pool(name="tpsum", bufs=6))
        o_psum = ctx.enter_context(tc.psum_pool(name="opsum", bufs=2))
        ctx.enter_context(tc.manual_schedule())

        ident = const.tile([P, P], F32)
        one = const.tile([P, 1], F32)
        warm = const.tile([P, 1], F32)
        xs = const.tile([P, ROW_TILES, DIM], BF16)
        xh = const.tile([P, X_COLS], F32)
        rs = const.tile([P, X_COLS], F32)
        rec = const.tile([P, X_COLS], F32)
        xq = const.tile([P, X_COLS], BF16, align_bytes=64)
        x_codes = const.tile([P, PASSES * DIM], U32, align_bytes=64)
        x_scales = const.tile([P, PASSES * DIM], U8, align_bytes=64)

        xs_pairs = xs[:].rearrange("p (c e) d -> p c (e d)", e=2)
        for part in range(2):
            chunks = slice(part * CHUNKS // 2, (part + 1) * CHUNKS // 2)
            nc.sync.dma_start(out=xs_pairs[:, chunks, :], in_=x_view[:, chunks, :])
        a_tiles = []
        for c in range(CHUNKS):
            a_sb = a_pool.tile([P, 2, N], BF16)
            a_tiles.append(a_sb)
            if c in (0, CHUNKS - 1):
                for e in range(2):
                    nc.sync.dma_start(out=a_sb[:, e, :], in_=a_view[:, c, e, :])
            else:
                nc.sync.dma_start(out=a_sb[:], in_=a_view[:, c, :, :])

        make_identity(nc, ident[:])
        nc.vector.memset(one[:], 1.0)
        nc.scalar.activation(out=warm[:], in_=one[:], func=ACT.Abs_reciprocal_sqrt)

        xs_flat = xs[:].rearrange("p n d -> p (n d)")
        half = X_COLS // 2
        quarter = X_COLS // 4
        for part in range(2):
            cols = slice(part * half, (part + 1) * half)
            nc.scalar.activation(out=xh[:, cols], in_=xs_flat[:, cols], func=ACT.Square)
            tiles = slice(part * ROW_TILES // 2, (part + 1) * ROW_TILES // 2)
            x_rows = xs[:, tiles, :].rearrange("p (g slot) d -> p g d slot", slot=4)
            nc.vector.tensor_tensor(
                out=xq[:, cols].rearrange("p (g d slot) -> p g d slot", g=PASSES // 2, slot=4),
                in0=x_rows,
                in1=x_rows,
                op=ALU.mult,
            )

        def reciprocal_step(step, q):
            cols = slice(q * quarter, (q + 1) * quarter)
            if step == "rsqrt":
                nc.scalar.activation(
                    out=rs[:, cols], in_=xh[:, cols], func=ACT.Abs_reciprocal_sqrt, bias=1.0, scale=1.0
                )
            else:
                nc.scalar.activation(out=rec[:, cols], in_=rs[:, cols], func=ACT.Square)

        reciprocal_step("rsqrt", 0)
        reciprocal_step("rsqrt", 1)
        reciprocal_step("square", 0)
        reciprocal_step("square", 1)

        grouped = {}
        codes = {}
        scales = {}
        acc = {}
        prods = {}

        def transposes_and_copies(n):
            a32 = a_tiles[n // 2][:, n % 2, :].bitcast(F32)
            grp = g_pool.tile([P, N], BF16, align_bytes=64)
            grouped[n] = grp
            for h in range(2):
                tp = t_psum.tile([P, BANK], F32)
                for j in range(4):
                    w = 4 * h + j
                    nc.tensor.transpose(tp[:, j * P : (j + 1) * P], a32[:, w * P : (w + 1) * P], ident[:])
                dst = grp[:, 2 * h * BANK : 2 * (h + 1) * BANK].bitcast(F32).rearrange("p (g i u) -> p g i u", g=2, u=2)
                src = tp[:].rearrange("p (g u i) -> p g i u", g=2, u=2)
                bank = 2 * n + h
                if bank in VECTOR_BANKS:
                    nc.vector.tensor_copy(out=dst, in_=src)
                else:
                    nc.scalar.copy(out=dst, in_=src)
                if bank in RECIPROCAL_AFTER_BANK:
                    reciprocal_step(RECIPROCAL_AFTER_BANK[bank][0], RECIPROCAL_AFTER_BANK[bank][1])

        def quantise(n, pieces):
            cd = q_pool.tile([P, PASSES * P], U32, align_bytes=64)
            sc = q_pool.tile([P, PASSES * P], U8, align_bytes=64)
            codes[n] = cd
            scales[n] = sc
            width = PASSES * P // pieces
            for piece in range(pieces):
                cols = slice(piece * width, (piece + 1) * width)
                nc.vector.quantize_mx(
                    out=cd[:, cols].bitcast(FP8X4),
                    scales=sc[:, cols],
                    in_=grouped[n][:, 4 * piece * width : 4 * (piece + 1) * width],
                )

        def products(c):
            ps = o_psum.tile([P, 2 * DIM], F32)
            acc[c] = ps
            for e in range(2):
                n = 2 * c + e
                for g in range(PASSES):
                    cols = slice(g * P, (g + 1) * P)
                    nc.tensor.matmul_mx(
                        out=ps[:, e * DIM : (e + 1) * DIM],
                        lhsT=codes[n][:, cols].bitcast(FP8X4),
                        lhsT_scale=scales[n][:, cols],
                        rhs=x_codes[:, cols].bitcast(FP8X4),
                        rhs_scale=x_scales[:, cols],
                        start=(g == 0),
                        stop=(g == PASSES - 1),
                    )

        def divide(c):
            cols = slice(2 * c * DIM, 2 * (c + 1) * DIM)
            prod = p_pool.tile([P, 2 * DIM], F32)
            prods[c] = prod
            nc.vector.tensor_tensor(out=prod[:], in0=acc[c][:], in1=rec[:, cols], op=ALU.mult)

        def subtract_and_store(c):
            cols = slice(2 * c * DIM, 2 * (c + 1) * DIM)
            res = r_pool.tile([P, 2 * DIM], F32)
            nc.vector.tensor_tensor(out=res[:], in0=prods[c][:], in1=xs_flat[:, cols], op=ALU.subtract)
            nc.sync.dma_start(out=out_view[:, c, :], in_=res[:])

        for c in range(CHUNKS):
            transposes_and_copies(2 * c)
            if c == 0:
                nc.vector.quantize_mx(out=x_codes[:].bitcast(FP8X4), scales=x_scales[:], in_=xq[:])
            transposes_and_copies(2 * c + 1)
            if 1 <= c <= LAST_WOVEN:
                products(c - 1)
            if c == CHUNKS - 1:
                products(c - 2)
                quantise(2 * c, 1)
                divide(c - 2)
                quantise(2 * c + 1, 2)
            else:
                if c >= 2:
                    divide(c - 2)
                quantise(2 * c, 1)
                if 2 <= c <= LAST_WOVEN:
                    subtract_and_store(c - 2)
                quantise(2 * c + 1, 1)
        products(CHUNKS - 2)
        products(CHUNKS - 1)
        subtract_and_store(CHUNKS - 4)
        divide(CHUNKS - 2)
        subtract_and_store(CHUNKS - 3)
        divide(CHUNKS - 1)
        subtract_and_store(CHUNKS - 2)
        subtract_and_store(CHUNKS - 1)
